import numpy as np
import ml_dtypes


def mxq(x, axis, fmt="e4m3"):
    dtype, down = {"e4m3": (ml_dtypes.float8_e4m3fn, 7), "e5m2": (ml_dtypes.float8_e5m2, 14)}[fmt]
    v = np.moveaxis(np.asarray(x, np.float32).astype(ml_dtypes.bfloat16).astype(np.float64), axis, -1)
    blocks = v.reshape(v.shape[:-1] + (-1, 32))
    amax = np.abs(blocks).max(-1, keepdims=True)
    byte = np.maximum(np.where(amax > 0, np.frexp(amax)[1] - 1 + 127, 0) - down, 1)
    scale = np.exp2(byte - 127.0)
    codes = (blocks / scale).astype(np.float32).astype(dtype).astype(np.float64)
    return np.moveaxis((codes * scale).reshape(v.shape), -1, axis)


WIDE = False


def mx_kscale(k):
    if not WIDE:
        return np.ones(k)
    levels = np.array([10, -10, 5, -5, 0])
    a = np.random.permutation(np.resize(levels, k // 512 * 4)).reshape(k // 512, 4)
    idx = np.arange(k)
    return np.exp2(a[idx // 512, idx % 128 // 32])


BF16 = ml_dtypes.bfloat16


def bf(x):
    return np.asarray(x, np.float32).astype(BF16)


def f64(x):
    return np.asarray(x).astype(np.float64)


B_, S, D_IN, D_OUT, N, RANK, ALPHA = 1, 128, 512, 1024, 32, 16, 32
NR = N * RANK
SCALE = ALPHA / RANK


def setup_inputs():
    s, t = mx_kscale(D_IN), mx_kscale(NR)
    tn = t.reshape(N, RANK)
    return {"x": bf(np.random.standard_normal((B_, S, D_IN)) * s),
            "lora_A": bf(np.random.standard_normal((N, RANK, D_IN)) / np.sqrt(D_IN) / s * tn[:, :, None]),
            "lora_B": bf(np.random.standard_normal((N, D_OUT, RANK)) / np.sqrt(RANK) / tn[:, None, :]),
            "W": bf(np.random.standard_normal((D_OUT, D_IN)) / np.sqrt(D_IN) / s),
            "bias": bf(np.random.standard_normal(D_OUT) * 0.3),
            "lora_weights": bf((1.0 + 0.5 * np.random.standard_normal(N)) * 2.0 / N)}


def reference(x, lora_A, lora_B, W, bias, lora_weights):
    xq = mxq(f64(x), 2, "e4m3")
    h = xq @ mxq(f64(lora_A).reshape(NR, D_IN), 1, "e4m3").T
    coef = (SCALE * f64(lora_weights))[:, None, None]
    bc = (f64(lora_B) * coef).transpose(1, 0, 2).reshape(D_OUT, NR)
    lora_out = mxq(h, 2, "e4m3") @ mxq(bc, 1, "e4m3").T
    base = (xq @ mxq(f64(W), 1, "e4m3").T) + f64(bias)
    return base + lora_out

@@ -1,0 +1,244 @@
+from contextlib import ExitStack
+
+import concourse.mybir as mybir
+from concourse.masks import make_identity
+
+F32 = mybir.dt.float32
+BF16 = mybir.dt.bfloat16
+U32 = mybir.dt.uint32
+U8 = mybir.dt.uint8
+FP8X4 = mybir.dt.float8_e4m3fn_x4
+
+P = 128
+D_IN = 512
+D_OUT = 1024
+ADAPTERS = 32
+RANK = 16
+LORA_SCALE = 2.0
+PACK = 4
+HALVES = 2
+BLOCKS_PER_BANK = 2
+O_PER_PARTITION = D_OUT // P
+N_TILE = 512
+OUT_BANKS = D_OUT // N_TILE
+L_PER_BANK = O_PER_PARTITION // OUT_BANKS
+B_CHUNKS = 4
+CHUNK_ADAPTERS = ADAPTERS // B_CHUNKS
+BIAS_ROWS = 4
+WEIGHT_ROW = 4
+
+FLOPS = 2 * P * D_IN * (ADAPTERS * RANK + D_OUT) + 2 * P * ADAPTERS * RANK * D_OUT
+
+
+def contraction_to_partitions(nc, banks, ident, blocks, grouped_words):
+    bank_tiles = []
+    for first in range(0, len(blocks), BLOCKS_PER_BANK):
+        bank = banks.tile([P, BLOCKS_PER_BANK, HALVES, P], F32, tag="bank")
+        bank_tiles.append(bank)
+    for u in range(HALVES):
+        for b in range(len(blocks)):
+            bank = bank_tiles[b // BLOCKS_PER_BANK]
+            nc.tensor.transpose(bank[:, b % BLOCKS_PER_BANK, u, :], blocks[b][u], ident[:])
+    for i, bank in enumerate(bank_tiles):
+        first = i * BLOCKS_PER_BANK
+        count = min(BLOCKS_PER_BANK, len(blocks) - first)
+        copy = nc.scalar.copy if i % 2 == 0 else nc.vector.tensor_copy
+        copy(
+            out=grouped_words[:, first * P : (first + count) * P, :].rearrange(
+                "p (b c) u -> p b c u", c=P
+            ),
+            in_=bank[:, 0:count].rearrange("p b u c -> p b c u"),
+        )
+
+
+def row_blocks(raw):
+    words = raw[:].bitcast(F32).rearrange("p (b u w) -> p b u w", u=HALVES, w=P)
+    return [[words[:, b, u, :] for u in range(HALVES)] for b in range(words.shape[1])]
+
+
+def as_grouped_words(grouped):
+    return grouped[:].bitcast(F32).rearrange("p (c u) -> p c u", u=HALVES)
+
+
+def tile_replaced_compose_lora_pa_s_kernel(
+    tc, x, lora_A, lora_B, W, bias, lora_weights, out
+):
+    nc = tc.nc
+    with ExitStack() as pools:
+        keep = pools.enter_context(tc.tile_pool(name="keep", bufs=1))
+        banks = pools.enter_context(tc.psum_pool(name="banks", bufs=5))
+        sums = pools.enter_context(tc.psum_pool(name="sums", bufs=1))
+
+        x_raw = keep.tile([P, D_IN], BF16)
+        nc.sync.dma_start(out=x_raw[:], in_=x.flatten_outer_dims())
+        a_raw = keep.tile([P, PACK * D_IN], BF16)
+        nc.sync.dma_start(
+            out=a_raw[:].rearrange("m (u r) -> m u r", u=HALVES),
+            in_=lora_A.flatten_outer_dims().rearrange("(u m e) d -> m u (e d)", u=HALVES, e=2),
+        )
+        b_raw = []
+        for c in range(B_CHUNKS):
+            chunk = keep.tile([P, CHUNK_ADAPTERS, O_PER_PARTITION * RANK], BF16, name="b_raw%d" % c)
+            nc.sync.dma_start(
+                out=chunk[:],
+                in_=lora_B[c * CHUNK_ADAPTERS : (c + 1) * CHUNK_ADAPTERS].rearrange(
+                    "n (p l) r -> p n (l r)", l=O_PER_PARTITION
+                ),
+            )
+            b_raw.append(chunk)
+        w_raw = []
+        w_rows = W.rearrange("(p l) d -> p (l d)", l=O_PER_PARTITION)
+        for g in range(OUT_BANKS):
+            chunk = keep.tile([P, L_PER_BANK * D_IN], BF16, name="w_raw%d" % g)
+            nc.sync.dma_start(
+                out=chunk[:], in_=w_rows[:, g * L_PER_BANK * D_IN : (g + 1) * L_PER_BANK * D_IN]
+            )
+            w_raw.append(chunk)
+
+        ident = keep.tile([P, P], F32)
+        make_identity(nc, ident[:])
+
+        rows = keep.tile([P, 2 * P], BF16)
+        nc.vector.memset(rows[:].bitcast(F32), 0.0)
+        nc.scalar.dma_start(
+            out=rows[0:BIAS_ROWS, :], in_=bias.rearrange("(i c) -> i c", i=BIAS_ROWS)
+        )
+        nc.scalar.dma_start(
+            out=rows[WEIGHT_ROW : WEIGHT_ROW + 1, 0:ADAPTERS],
+            in_=lora_weights.rearrange("(o n) -> o n", o=1),
+        )
+        rows_bank = banks.tile([P, P], F32, tag="bank")
+        nc.tensor.transpose(rows_bank[:], rows[:].bitcast(F32), ident[:])
+        columns = keep.tile([P, WEIGHT_ROW + 1], F32)
+        nc.vector.tensor_copy(out=columns[:], in_=rows_bank[:, 0 : WEIGHT_ROW + 1])
+        weight_bank = banks.tile([P, P], F32, tag="bank")
+        nc.tensor.transpose(
+            weight_bank[:], columns[:, WEIGHT_ROW : WEIGHT_ROW + 1].to_broadcast([P, P]), ident[:]
+        )
+        coef = keep.tile([P, ADAPTERS, RANK], BF16)
+        nc.scalar.mul(
+            out=coef[:],
+            in_=weight_bank[:, 0 : ADAPTERS // 2]
+            .bitcast(BF16)
+            .unsqueeze(2)
+            .to_broadcast([P, ADAPTERS, RANK]),
+            mul=LORA_SCALE,
+        )
+        bias_bank = banks.tile([P, BIAS_ROWS, P], F32, tag="bank")
+        for i in range(BIAS_ROWS):
+            nc.tensor.transpose(
+                bias_bank[:, i, :], columns[:, i : i + 1].to_broadcast([P, P]), ident[:]
+            )
+        bias_all = keep.tile([P, D_OUT], BF16)
+        nc.scalar.copy(
+            out=bias_all[:].bitcast(F32), in_=bias_bank[:].rearrange("p i w -> p (i w)")
+        )
+
+        x_grouped = keep.tile([P, P * PACK], BF16, align_bytes=64)
+        contraction_to_partitions(nc, banks, ident, row_blocks(x_raw), as_grouped_words(x_grouped))
+        x_codes = keep.tile([P, P], U32, align_bytes=64)
+        x_scales = keep.tile([P, P], U8, align_bytes=64)
+        nc.vector.quantize_mx(out=x_codes[:].bitcast(FP8X4), scales=x_scales[:], in_=x_grouped[:])
+
+        a_grouped = keep.tile([P, PACK * P * PACK], BF16, align_bytes=64)
+        contraction_to_partitions(nc, banks, ident, row_blocks(a_raw), as_grouped_words(a_grouped))
+        a_codes = keep.tile([P, PACK * P], U32, align_bytes=64)
+        a_scales = keep.tile([P, PACK * P], U8, align_bytes=64)
+        nc.vector.quantize_mx(out=a_codes[:].bitcast(FP8X4), scales=a_scales[:], in_=a_grouped[:])
+
+        h_bank = sums.tile([P, PACK, P], F32)
+        for t in range(PACK):
+            nc.tensor.matmul_mx(
+                out=h_bank[:, t, :],
+                lhsT=a_codes[:, t * P : (t + 1) * P].bitcast(FP8X4),
+                lhsT_scale=a_scales[:, t * P : (t + 1) * P],
+                rhs=x_codes[:].bitcast(FP8X4),
+                rhs_scale=x_scales[:],
+                start=True,
+                stop=True,
+            )
+        h_grouped = keep.tile([P, P * PACK], BF16, align_bytes=64)
+        nc.scalar.copy(
+            out=h_grouped[:].rearrange("p (s t) -> p s t", t=PACK),
+            in_=h_bank[:].rearrange("p t s -> p s t"),
+        )
+        h_codes = keep.tile([P, P], U32, align_bytes=64)
+        h_scales = keep.tile([P, P], U8, align_bytes=64)
+        nc.vector.quantize_mx(out=h_codes[:].bitcast(FP8X4), scales=h_scales[:], in_=h_grouped[:])
+
+        half_adapters = ADAPTERS // HALVES
+        bc = []
+        for u in range(HALVES):
+            half = keep.tile([P, O_PER_PARTITION * half_adapters * RANK], BF16, name="bc%d" % u)
+            bc.append(half)
+        for c in range(B_CHUNKS):
+            first = c * CHUNK_ADAPTERS
+            in_half = first % half_adapters
+            nc.vector.tensor_tensor(
+                out=bc[first // half_adapters][:].rearrange(
+                    "p (l n r) -> p l n r", l=O_PER_PARTITION, r=RANK
+                )[:, :, in_half : in_half + CHUNK_ADAPTERS, :],
+                in0=b_raw[c][:].rearrange("p n (l r) -> p l n r", r=RANK),
+                in1=coef[:, first : first + CHUNK_ADAPTERS, :]
+                .unsqueeze(1)
+                .to_broadcast([P, O_PER_PARTITION, CHUNK_ADAPTERS, RANK]),
+                op=mybir.AluOpType.mult,
+            )
+        bc_words = [half[:].bitcast(F32).rearrange("p (l w) -> p l w", w=P) for half in bc]
+        bc_blocks = [[bc_words[u][:, l, :] for u in range(HALVES)] for l in range(O_PER_PARTITION)]
+        b_grouped = keep.tile([P, D_OUT * PACK], BF16, align_bytes=64)
+        contraction_to_partitions(nc, banks, ident, bc_blocks, as_grouped_words(b_grouped))
+        b_codes = keep.tile([P, D_OUT], U32, align_bytes=64)
+        b_scales = keep.tile([P, D_OUT], U8, align_bytes=64)
+        for g in range(OUT_BANKS):
+            cols = slice(g * N_TILE, (g + 1) * N_TILE)
+            nc.vector.quantize_mx(
+                out=b_codes[:, cols].bitcast(FP8X4),
+                scales=b_scales[:, cols],
+                in_=b_grouped[:, g * N_TILE * PACK : (g + 1) * N_TILE * PACK],
+            )
+
+        w_grouped = keep.tile([P, D_OUT * PACK], BF16, align_bytes=64)
+        w_codes = keep.tile([P, D_OUT], U32, align_bytes=64)
+        w_scales = keep.tile([P, D_OUT], U8, align_bytes=64)
+        for g in range(OUT_BANKS):
+            cols = slice(g * N_TILE, (g + 1) * N_TILE)
+            contraction_to_partitions(
+                nc, banks, ident, row_blocks(w_raw[g]), as_grouped_words(w_grouped)[:, cols, :]
+            )
+            nc.vector.quantize_mx(
+                out=w_codes[:, cols].bitcast(FP8X4),
+                scales=w_scales[:, cols],
+                in_=w_grouped[:, g * N_TILE * PACK : (g + 1) * N_TILE * PACK],
+            )
+
+        out_sb = keep.tile([P, D_OUT], F32)
+        for g in range(OUT_BANKS):
+            cols = slice(g * N_TILE, (g + 1) * N_TILE)
+            acc = sums.tile([P, N_TILE], F32, name="acc%d" % g)
+            nc.tensor.matmul_mx(
+                out=acc[:],
+                lhsT=h_codes[:].bitcast(FP8X4),
+                lhsT_scale=h_scales[:],
+                rhs=b_codes[:, cols].bitcast(FP8X4),
+                rhs_scale=b_scales[:, cols],
+                start=True,
+                stop=False,
+            )
+            nc.tensor.matmul_mx(
+                out=acc[:],
+                lhsT=x_codes[:].bitcast(FP8X4),
+                lhsT_scale=x_scales[:],
+                rhs=w_codes[:, cols].bitcast(FP8X4),
+                rhs_scale=w_scales[:, cols],
+                start=False,
+                stop=True,
+            )
+            ls = slice(g * L_PER_BANK, (g + 1) * L_PER_BANK)
+            nc.vector.tensor_tensor(
+                out=out_sb[:].rearrange("s (p l) -> s p l", l=O_PER_PARTITION)[:, :, ls],
+                in0=acc[:].rearrange("s (l p) -> s p l", p=P),
+                in1=bias_all[:].rearrange("s (p l) -> s p l", l=O_PER_PARTITION)[:, :, ls],
+                op=mybir.AluOpType.add,
+            )
+        nc.sync.dma_start(out=out.flatten_outer_dims(), in_=out_sb[:])

@@ -18,19 +18,20 @@ LORA_SCALE = 2.0
 PACK = 4
 HALVES = 2
 BLOCKS_PER_BANK = 2
+PSUM_BANKS = 8
 O_PER_PARTITION = D_OUT // P
-N_TILE = 512
-OUT_BANKS = D_OUT // N_TILE
-L_PER_BANK = O_PER_PARTITION // OUT_BANKS
-B_CHUNKS = 4
-CHUNK_ADAPTERS = ADAPTERS // B_CHUNKS
+HALF_ADAPTERS = ADAPTERS // HALVES
+CHUNK_ADAPTERS = 8
+OUT_CHUNKS = 4
+N_TILE = D_OUT // OUT_CHUNKS
+ROWS_PER_PARTITION = N_TILE // P
 BIAS_ROWS = 4
 WEIGHT_ROW = 4
 
 FLOPS = 2 * P * D_IN * (ADAPTERS * RANK + D_OUT) + 2 * P * ADAPTERS * RANK * D_OUT
 
 
-def contraction_to_partitions(nc, banks, ident, blocks, grouped_words):
+def contraction_to_partitions(nc, banks, ident, blocks, places):
     bank_tiles = []
     for first in range(0, len(blocks), BLOCKS_PER_BANK):
         bank = banks.tile([P, BLOCKS_PER_BANK, HALVES, P], F32, tag="bank")
@@ -42,12 +43,10 @@ def contraction_to_partitions(nc, banks, ident, blocks, grouped_words):
     for i, bank in enumerate(bank_tiles):
         first = i * BLOCKS_PER_BANK
         count = min(BLOCKS_PER_BANK, len(blocks) - first)
-        copy = nc.scalar.copy if i % 2 == 0 else nc.vector.tensor_copy
+        copy = nc.scalar.copy if 2 * i < len(bank_tiles) else nc.vector.tensor_copy
         copy(
-            out=grouped_words[:, first * P : (first + count) * P, :].rearrange(
-                "p (b c) u -> p b c u", c=P
-            ),
-            in_=bank[:, 0:count].rearrange("p b u c -> p b c u"),
+            out=places[:, :, first : first + count, :],
+            in_=bank[:, 0:count].rearrange("w b u c -> w c b u"),
         )
 
 
@@ -56,19 +55,24 @@ def row_blocks(raw):
     return [[words[:, b, u, :] for u in range(HALVES)] for b in range(words.shape[1])]
 
 
-def as_grouped_words(grouped):
-    return grouped[:].bitcast(F32).rearrange("p (c u) -> p c u", u=HALVES)
-
-
 def tile_replaced_compose_lora_pa_s_kernel(
     tc, x, lora_A, lora_B, W, bias, lora_weights, out
 ):
     nc = tc.nc
-    with ExitStack() as pools:
-        keep = pools.enter_context(tc.tile_pool(name="keep", bufs=1))
-        banks = pools.enter_context(tc.psum_pool(name="banks", bufs=5))
-        sums = pools.enter_context(tc.psum_pool(name="sums", bufs=1))
+    with ExitStack() as stack:
+        keep = stack.enter_context(tc.tile_pool(name="keep", bufs=1))
+        banks = stack.enter_context(tc.psum_pool(name="banks", bufs=PSUM_BANKS))
+        stack.enter_context(tc.manual_schedule())
 
+        rows = keep.tile([P, 2 * P], BF16)
+        nc.vector.memset(rows[:].bitcast(F32), 0.0)
+        nc.sync.dma_start(
+            out=rows[0:BIAS_ROWS, :], in_=bias.rearrange("(i c) -> i c", i=BIAS_ROWS)
+        )
+        nc.sync.dma_start(
+            out=rows[WEIGHT_ROW : WEIGHT_ROW + 1, 0:ADAPTERS],
+            in_=lora_weights.rearrange("(o n) -> o n", o=1),
+        )
         x_raw = keep.tile([P, D_IN], BF16)
         nc.sync.dma_start(out=x_raw[:], in_=x.flatten_outer_dims())
         a_raw = keep.tile([P, PACK * D_IN], BF16)
@@ -77,52 +81,57 @@ def tile_replaced_compose_lora_pa_s_kernel(
             in_=lora_A.flatten_outer_dims().rearrange("(u m e) d -> m u (e d)", u=HALVES, e=2),
         )
         b_raw = []
-        for c in range(B_CHUNKS):
-            chunk = keep.tile([P, CHUNK_ADAPTERS, O_PER_PARTITION * RANK], BF16, name="b_raw%d" % c)
+        for first in range(0, ADAPTERS, CHUNK_ADAPTERS):
+            chunk = keep.tile(
+                [P, CHUNK_ADAPTERS, O_PER_PARTITION * RANK], BF16, name="b_raw%d" % first
+            )
             nc.sync.dma_start(
                 out=chunk[:],
-                in_=lora_B[c * CHUNK_ADAPTERS : (c + 1) * CHUNK_ADAPTERS].rearrange(
+                in_=lora_B[first : first + CHUNK_ADAPTERS].rearrange(
                     "n (p l) r -> p n (l r)", l=O_PER_PARTITION
                 ),
             )
             b_raw.append(chunk)
         w_raw = []
-        w_rows = W.rearrange("(p l) d -> p (l d)", l=O_PER_PARTITION)
-        for g in range(OUT_BANKS):
-            chunk = keep.tile([P, L_PER_BANK * D_IN], BF16, name="w_raw%d" % g)
+        for g in range(OUT_CHUNKS):
+            chunk = keep.tile([P, ROWS_PER_PARTITION * D_IN], BF16, name="w_raw%d" % g)
             nc.sync.dma_start(
-                out=chunk[:], in_=w_rows[:, g * L_PER_BANK * D_IN : (g + 1) * L_PER_BANK * D_IN]
+                out=chunk[:],
+                in_=W[g * N_TILE : (g + 1) * N_TILE, :].rearrange(
+                    "(q j) d -> q (j d)", j=ROWS_PER_PARTITION
+                ),
             )
             w_raw.append(chunk)
 
         ident = keep.tile([P, P], F32)
         make_identity(nc, ident[:])
 
-        rows = keep.tile([P, 2 * P], BF16)
-        nc.vector.memset(rows[:].bitcast(F32), 0.0)
-        nc.scalar.dma_start(
-            out=rows[0:BIAS_ROWS, :], in_=bias.rearrange("(i c) -> i c", i=BIAS_ROWS)
-        )
-        nc.scalar.dma_start(
-            out=rows[WEIGHT_ROW : WEIGHT_ROW + 1, 0:ADAPTERS],
-            in_=lora_weights.rearrange("(o n) -> o n", o=1),
-        )
         rows_bank = banks.tile([P, P], F32, tag="bank")
         nc.tensor.transpose(rows_bank[:], rows[:].bitcast(F32), ident[:])
         columns = keep.tile([P, WEIGHT_ROW + 1], F32)
         nc.vector.tensor_copy(out=columns[:], in_=rows_bank[:, 0 : WEIGHT_ROW + 1])
+
+        x_grouped = keep.tile([P, P * PACK], BF16, align_bytes=64)
+        contraction_to_partitions(
+            nc,
+            banks,
+            ident,
+            row_blocks(x_raw),
+            x_grouped[:].bitcast(F32).rearrange("w (b c u) -> w c b u", b=1, u=HALVES),
+        )
+
         weight_bank = banks.tile([P, P], F32, tag="bank")
         nc.tensor.transpose(
             weight_bank[:], columns[:, WEIGHT_ROW : WEIGHT_ROW + 1].to_broadcast([P, P]), ident[:]
         )
         coef = keep.tile([P, ADAPTERS, RANK], BF16)
-        nc.scalar.mul(
+        nc.vector.tensor_scalar_mul(
             out=coef[:],
-            in_=weight_bank[:, 0 : ADAPTERS // 2]
+            in0=weight_bank[:, 0 : ADAPTERS // 2]
             .bitcast(BF16)
             .unsqueeze(2)
             .to_broadcast([P, ADAPTERS, RANK]),
-            mul=LORA_SCALE,
+            scalar1=LORA_SCALE,
         )
         bias_bank = banks.tile([P, BIAS_ROWS, P], F32, tag="bank")
         for i in range(BIAS_ROWS):
@@ -134,19 +143,44 @@ def tile_replaced_compose_lora_pa_s_kernel(
             out=bias_all[:].bitcast(F32), in_=bias_bank[:].rearrange("p i w -> p (i w)")
         )
 
-        x_grouped = keep.tile([P, P * PACK], BF16, align_bytes=64)
-        contraction_to_partitions(nc, banks, ident, row_blocks(x_raw), as_grouped_words(x_grouped))
         x_codes = keep.tile([P, P], U32, align_bytes=64)
         x_scales = keep.tile([P, P], U8, align_bytes=64)
         nc.vector.quantize_mx(out=x_codes[:].bitcast(FP8X4), scales=x_scales[:], in_=x_grouped[:])
 
         a_grouped = keep.tile([P, PACK * P * PACK], BF16, align_bytes=64)
-        contraction_to_partitions(nc, banks, ident, row_blocks(a_raw), as_grouped_words(a_grouped))
+        contraction_to_partitions(
+            nc,
+            banks,
+            ident,
+            row_blocks(a_raw),
+            a_grouped[:].bitcast(F32).rearrange("w (b c u) -> w c b u", b=PACK, u=HALVES),
+        )
         a_codes = keep.tile([P, PACK * P], U32, align_bytes=64)
         a_scales = keep.tile([P, PACK * P], U8, align_bytes=64)
         nc.vector.quantize_mx(out=a_codes[:].bitcast(FP8X4), scales=a_scales[:], in_=a_grouped[:])
 
-        h_bank = sums.tile([P, PACK, P], F32)
+        bc = []
+        for u in range(HALVES):
+            half = keep.tile([P, O_PER_PARTITION * HALF_ADAPTERS * RANK], BF16, name="bc%d" % u)
+            bc.append(half)
+
+        def scale_half(u):
+            for in_half in range(0, HALF_ADAPTERS, CHUNK_ADAPTERS):
+                first = u * HALF_ADAPTERS + in_half
+                nc.vector.tensor_tensor(
+                    out=bc[u][:].rearrange("p (l n r) -> p l n r", l=O_PER_PARTITION, r=RANK)[
+                        :, :, in_half : in_half + CHUNK_ADAPTERS, :
+                    ],
+                    in0=b_raw[first // CHUNK_ADAPTERS][:].rearrange("p n (l r) -> p l n r", r=RANK),
+                    in1=coef[:, first : first + CHUNK_ADAPTERS, :]
+                    .unsqueeze(1)
+                    .to_broadcast([P, O_PER_PARTITION, CHUNK_ADAPTERS, RANK]),
+                    op=mybir.AluOpType.mult,
+                )
+
+        scale_half(0)
+
+        h_bank = banks.tile([P, PACK, P], F32, tag="bank")
         for t in range(PACK):
             nc.tensor.matmul_mx(
                 out=h_bank[:, t, :],
@@ -166,56 +200,50 @@ def tile_replaced_compose_lora_pa_s_kernel(
         h_scales = keep.tile([P, P], U8, align_bytes=64)
         nc.vector.quantize_mx(out=h_codes[:].bitcast(FP8X4), scales=h_scales[:], in_=h_grouped[:])
 
-        half_adapters = ADAPTERS // HALVES
-        bc = []
-        for u in range(HALVES):
-            half = keep.tile([P, O_PER_PARTITION * half_adapters * RANK], BF16, name="bc%d" % u)
-            bc.append(half)
-        for c in range(B_CHUNKS):
-            first = c * CHUNK_ADAPTERS
-            in_half = first % half_adapters
-            nc.vector.tensor_tensor(
-                out=bc[first // half_adapters][:].rearrange(
-                    "p (l n r) -> p l n r", l=O_PER_PARTITION, r=RANK
-                )[:, :, in_half : in_half + CHUNK_ADAPTERS, :],
-                in0=b_raw[c][:].rearrange("p n (l r) -> p l n r", r=RANK),
-                in1=coef[:, first : first + CHUNK_ADAPTERS, :]
-                .unsqueeze(1)
-                .to_broadcast([P, O_PER_PARTITION, CHUNK_ADAPTERS, RANK]),
-                op=mybir.AluOpType.mult,
-            )
+        scale_half(1)
+
         bc_words = [half[:].bitcast(F32).rearrange("p (l w) -> p l w", w=P) for half in bc]
-        bc_blocks = [[bc_words[u][:, l, :] for u in range(HALVES)] for l in range(O_PER_PARTITION)]
         b_grouped = keep.tile([P, D_OUT * PACK], BF16, align_bytes=64)
-        contraction_to_partitions(nc, banks, ident, bc_blocks, as_grouped_words(b_grouped))
-        b_codes = keep.tile([P, D_OUT], U32, align_bytes=64)
-        b_scales = keep.tile([P, D_OUT], U8, align_bytes=64)
-        for g in range(OUT_BANKS):
-            cols = slice(g * N_TILE, (g + 1) * N_TILE)
-            nc.vector.quantize_mx(
-                out=b_codes[:, cols].bitcast(FP8X4),
-                scales=b_scales[:, cols],
-                in_=b_grouped[:, g * N_TILE * PACK : (g + 1) * N_TILE * PACK],
-            )
+        contraction_to_partitions(
+            nc,
+            banks,
+            ident,
+            [[bc_words[u][:, l, :] for u in range(HALVES)] for l in range(O_PER_PARTITION)],
+            b_grouped[:].bitcast(F32).rearrange("w (c b u) -> w c b u", b=O_PER_PARTITION, u=HALVES),
+        )
 
         w_grouped = keep.tile([P, D_OUT * PACK], BF16, align_bytes=64)
-        w_codes = keep.tile([P, D_OUT], U32, align_bytes=64)
-        w_scales = keep.tile([P, D_OUT], U8, align_bytes=64)
-        for g in range(OUT_BANKS):
-            cols = slice(g * N_TILE, (g + 1) * N_TILE)
+        for g in range(OUT_CHUNKS):
             contraction_to_partitions(
-                nc, banks, ident, row_blocks(w_raw[g]), as_grouped_words(w_grouped)[:, cols, :]
-            )
-            nc.vector.quantize_mx(
-                out=w_codes[:, cols].bitcast(FP8X4),
-                scales=w_scales[:, cols],
-                in_=w_grouped[:, g * N_TILE * PACK : (g + 1) * N_TILE * PACK],
+                nc,
+                banks,
+                ident,
+                row_blocks(w_raw[g]),
+                w_grouped[:, g * N_TILE * PACK : (g + 1) * N_TILE * PACK]
+                .bitcast(F32)
+                .rearrange("w (c b u) -> w c b u", b=ROWS_PER_PARTITION, u=HALVES),
             )
 
+        b_codes = keep.tile([P, D_OUT], U32, align_bytes=64)
+        b_scales = keep.tile([P, D_OUT], U8, align_bytes=64)
+        w_codes = keep.tile([P, D_OUT], U32, align_bytes=64)
+        w_scales = keep.tile([P, D_OUT], U8, align_bytes=64)
         out_sb = keep.tile([P, D_OUT], F32)
-        for g in range(OUT_BANKS):
+        out_rows = out.flatten_outer_dims()
+
+        def quantise_piece(g):
             cols = slice(g * N_TILE, (g + 1) * N_TILE)
-            acc = sums.tile([P, N_TILE], F32, name="acc%d" % g)
+            values = slice(g * N_TILE * PACK, (g + 1) * N_TILE * PACK)
+            nc.vector.quantize_mx(
+                out=b_codes[:, cols].bitcast(FP8X4), scales=b_scales[:, cols], in_=b_grouped[:, values]
+            )
+            nc.vector.quantize_mx(
+                out=w_codes[:, cols].bitcast(FP8X4), scales=w_scales[:, cols], in_=w_grouped[:, values]
+            )
+
+        def finish_piece(g):
+            cols = slice(g * N_TILE, (g + 1) * N_TILE)
+            acc = banks.tile([P, N_TILE], F32, tag="bank")
             nc.tensor.matmul_mx(
                 out=acc[:],
                 lhsT=h_codes[:].bitcast(FP8X4),
@@ -234,11 +262,13 @@ def tile_replaced_compose_lora_pa_s_kernel(
                 start=False,
                 stop=True,
             )
-            ls = slice(g * L_PER_BANK, (g + 1) * L_PER_BANK)
             nc.vector.tensor_tensor(
-                out=out_sb[:].rearrange("s (p l) -> s p l", l=O_PER_PARTITION)[:, :, ls],
-                in0=acc[:].rearrange("s (l p) -> s p l", p=P),
-                in1=bias_all[:].rearrange("s (p l) -> s p l", l=O_PER_PARTITION)[:, :, ls],
-                op=mybir.AluOpType.add,
+                out=out_sb[:, cols], in0=acc[:], in1=bias_all[:, cols], op=mybir.AluOpType.add
             )
-        nc.sync.dma_start(out=out.flatten_outer_dims(), in_=out_sb[:])
+            nc.sync.dma_start(out=out_rows[:, cols], in_=out_sb[:, cols])
+
+        quantise_piece(0)
+        for g in range(1, OUT_CHUNKS):
+            quantise_piece(g)
+            finish_piece(g - 1)
+        finish_piece(OUT_CHUNKS - 1)

@@ -31,23 +31,35 @@ WEIGHT_ROW = 4
 FLOPS = 2 * P * D_IN * (ADAPTERS * RANK + D_OUT) + 2 * P * ADAPTERS * RANK * D_OUT
 
 
-def contraction_to_partitions(nc, banks, ident, blocks, places):
+def banks_for(banks, blocks):
     bank_tiles = []
     for first in range(0, len(blocks), BLOCKS_PER_BANK):
         bank = banks.tile([P, BLOCKS_PER_BANK, HALVES, P], F32, tag="bank")
         bank_tiles.append(bank)
-    for u in range(HALVES):
-        for b in range(len(blocks)):
-            bank = bank_tiles[b // BLOCKS_PER_BANK]
-            nc.tensor.transpose(bank[:, b % BLOCKS_PER_BANK, u, :], blocks[b][u], ident[:])
+    return bank_tiles
+
+
+def transpose_half(nc, bank_tiles, ident, blocks, u):
+    for b in range(len(blocks)):
+        bank = bank_tiles[b // BLOCKS_PER_BANK]
+        nc.tensor.transpose(bank[:, b % BLOCKS_PER_BANK, u, :], blocks[b][u], ident[:])
+
+
+def leave_banks(bank_tiles, n_blocks, places, copies):
     for i, bank in enumerate(bank_tiles):
         first = i * BLOCKS_PER_BANK
-        count = min(BLOCKS_PER_BANK, len(blocks) - first)
-        copy = nc.scalar.copy if 2 * i < len(bank_tiles) else nc.vector.tensor_copy
-        copy(
+        count = min(BLOCKS_PER_BANK, n_blocks - first)
+        copies[i * len(copies) // len(bank_tiles)](
             out=places[:, :, first : first + count, :],
             in_=bank[:, 0:count].rearrange("w b u c -> w c b u"),
         )
+
+
+def contraction_to_partitions(nc, banks, ident, blocks, places):
+    bank_tiles = banks_for(banks, blocks)
+    for u in range(HALVES):
+        transpose_half(nc, bank_tiles, ident, blocks, u)
+    leave_banks(bank_tiles, len(blocks), places, [nc.scalar.copy])
 
 
 def row_blocks(raw):
@@ -94,14 +106,14 @@ def tile_replaced_compose_lora_pa_s_kernel(
             b_raw.append(chunk)
         w_raw = []
         for g in range(OUT_CHUNKS):
-            chunk = keep.tile([P, ROWS_PER_PARTITION * D_IN], BF16, name="w_raw%d" % g)
+            piece = keep.tile([P, ROWS_PER_PARTITION * D_IN], BF16, name="w_raw%d" % g)
             nc.sync.dma_start(
-                out=chunk[:],
+                out=piece[:],
                 in_=W[g * N_TILE : (g + 1) * N_TILE, :].rearrange(
                     "(q j) d -> q (j d)", j=ROWS_PER_PARTITION
                 ),
             )
-            w_raw.append(chunk)
+            w_raw.append(piece)
 
         ident = keep.tile([P, P], F32)
         make_identity(nc, ident[:])
@@ -133,16 +145,6 @@ def tile_replaced_compose_lora_pa_s_kernel(
             .to_broadcast([P, ADAPTERS, RANK]),
             scalar1=LORA_SCALE,
         )
-        bias_bank = banks.tile([P, BIAS_ROWS, P], F32, tag="bank")
-        for i in range(BIAS_ROWS):
-            nc.tensor.transpose(
-                bias_bank[:, i, :], columns[:, i : i + 1].to_broadcast([P, P]), ident[:]
-            )
-        bias_all = keep.tile([P, D_OUT], BF16)
-        nc.scalar.copy(
-            out=bias_all[:].bitcast(F32), in_=bias_bank[:].rearrange("p i w -> p (i w)")
-        )
-
         x_codes = keep.tile([P, P], U32, align_bytes=64)
         x_scales = keep.tile([P, P], U8, align_bytes=64)
         nc.vector.quantize_mx(out=x_codes[:].bitcast(FP8X4), scales=x_scales[:], in_=x_grouped[:])
@@ -155,14 +157,23 @@ def tile_replaced_compose_lora_pa_s_kernel(
             row_blocks(a_raw),
             a_grouped[:].bitcast(F32).rearrange("w (b c u) -> w c b u", b=PACK, u=HALVES),
         )
-        a_codes = keep.tile([P, PACK * P], U32, align_bytes=64)
-        a_scales = keep.tile([P, PACK * P], U8, align_bytes=64)
-        nc.vector.quantize_mx(out=a_codes[:].bitcast(FP8X4), scales=a_scales[:], in_=a_grouped[:])
+
+        bias_bank = banks.tile([P, BIAS_ROWS, P], F32, tag="bank")
+        for i in range(BIAS_ROWS):
+            nc.tensor.transpose(
+                bias_bank[:, i, :], columns[:, i : i + 1].to_broadcast([P, P]), ident[:]
+            )
+        bias_all = keep.tile([P, D_OUT], BF16)
+        nc.scalar.copy(
+            out=bias_all[:].bitcast(F32), in_=bias_bank[:].rearrange("p i w -> p (i w)")
+        )
 
         bc = []
         for u in range(HALVES):
             half = keep.tile([P, O_PER_PARTITION * HALF_ADAPTERS * RANK], BF16, name="bc%d" % u)
             bc.append(half)
+        bc_words = [half[:].bitcast(F32).rearrange("p (l w) -> p l w", w=P) for half in bc]
+        bc_blocks = [[bc_words[u][:, l, :] for u in range(HALVES)] for l in range(O_PER_PARTITION)]
 
         def scale_half(u):
             for in_half in range(0, HALF_ADAPTERS, CHUNK_ADAPTERS):
@@ -179,7 +190,12 @@ def tile_replaced_compose_lora_pa_s_kernel(
                 )
 
         scale_half(0)
+        bc_banks = banks_for(banks, bc_blocks)
+        transpose_half(nc, bc_banks, ident, bc_blocks, 0)
 
+        a_codes = keep.tile([P, PACK * P], U32, align_bytes=64)
+        a_scales = keep.tile([P, PACK * P], U8, align_bytes=64)
+        nc.vector.quantize_mx(out=a_codes[:].bitcast(FP8X4), scales=a_scales[:], in_=a_grouped[:])
         h_bank = banks.tile([P, PACK, P], F32, tag="bank")
         for t in range(PACK):
             nc.tensor.matmul_mx(
@@ -196,20 +212,20 @@ def tile_replaced_compose_lora_pa_s_kernel(
             out=h_grouped[:].rearrange("p (s t) -> p s t", t=PACK),
             in_=h_bank[:].rearrange("p t s -> p s t"),
         )
+
+        scale_half(1)
+        transpose_half(nc, bc_banks, ident, bc_blocks, 1)
+
         h_codes = keep.tile([P, P], U32, align_bytes=64)
         h_scales = keep.tile([P, P], U8, align_bytes=64)
         nc.vector.quantize_mx(out=h_codes[:].bitcast(FP8X4), scales=h_scales[:], in_=h_grouped[:])
 
-        scale_half(1)
-
-        bc_words = [half[:].bitcast(F32).rearrange("p (l w) -> p l w", w=P) for half in bc]
         b_grouped = keep.tile([P, D_OUT * PACK], BF16, align_bytes=64)
-        contraction_to_partitions(
-            nc,
-            banks,
-            ident,
-            [[bc_words[u][:, l, :] for u in range(HALVES)] for l in range(O_PER_PARTITION)],
+        leave_banks(
+            bc_banks,
+            len(bc_blocks),
             b_grouped[:].bitcast(F32).rearrange("w (c b u) -> w c b u", b=O_PER_PARTITION, u=HALVES),
+            [nc.scalar.copy, nc.vector.tensor_copy],
         )
 
         w_grouped = keep.tile([P, D_OUT * PACK], BF16, align_bytes=64)

@@ -39,26 +39,32 @@ def banks_for(banks, blocks):
     return bank_tiles
 
 
-def transpose_half(nc, bank_tiles, ident, blocks, u):
-    for b in range(len(blocks)):
-        bank = bank_tiles[b // BLOCKS_PER_BANK]
-        nc.tensor.transpose(bank[:, b % BLOCKS_PER_BANK, u, :], blocks[b][u], ident[:])
+def dealt(n_banks, n_engines):
+    run = n_banks // n_engines
+    return [(e, e * run + i) for i in range(run) for e in range(n_engines)]
+
+
+def transpose_half(nc, bank_tiles, ident, blocks, u, n_engines):
+    for e, i in dealt(len(bank_tiles), n_engines):
+        first = i * BLOCKS_PER_BANK
+        for b in range(first, min(first + BLOCKS_PER_BANK, len(blocks))):
+            nc.tensor.transpose(bank_tiles[i][:, b - first, u, :], blocks[b][u], ident[:])
 
 
 def leave_banks(bank_tiles, n_blocks, places, copies):
-    for i, bank in enumerate(bank_tiles):
+    for e, i in dealt(len(bank_tiles), len(copies)):
         first = i * BLOCKS_PER_BANK
         count = min(BLOCKS_PER_BANK, n_blocks - first)
-        copies[i * len(copies) // len(bank_tiles)](
+        copies[e](
             out=places[:, :, first : first + count, :],
-            in_=bank[:, 0:count].rearrange("w b u c -> w c b u"),
+            in_=bank_tiles[i][:, 0:count].rearrange("w b u c -> w c b u"),
         )
 
 
 def contraction_to_partitions(nc, banks, ident, blocks, places):
     bank_tiles = banks_for(banks, blocks)
     for u in range(HALVES):
-        transpose_half(nc, bank_tiles, ident, blocks, u)
+        transpose_half(nc, bank_tiles, ident, blocks, u, 1)
     leave_banks(bank_tiles, len(blocks), places, [nc.scalar.copy])
 
 
@@ -76,17 +82,17 @@ def tile_replaced_compose_lora_pa_s_kernel(
         banks = stack.enter_context(tc.psum_pool(name="banks", bufs=PSUM_BANKS))
         stack.enter_context(tc.manual_schedule())
 
+        x_raw = keep.tile([P, D_IN], BF16)
+        nc.sync.dma_start(out=x_raw[:], in_=x.flatten_outer_dims())
         rows = keep.tile([P, 2 * P], BF16)
         nc.vector.memset(rows[:].bitcast(F32), 0.0)
-        nc.sync.dma_start(
-            out=rows[0:BIAS_ROWS, :], in_=bias.rearrange("(i c) -> i c", i=BIAS_ROWS)
-        )
         nc.sync.dma_start(
             out=rows[WEIGHT_ROW : WEIGHT_ROW + 1, 0:ADAPTERS],
             in_=lora_weights.rearrange("(o n) -> o n", o=1),
         )
-        x_raw = keep.tile([P, D_IN], BF16)
-        nc.sync.dma_start(out=x_raw[:], in_=x.flatten_outer_dims())
+        nc.sync.dma_start(
+            out=rows[0:BIAS_ROWS, :], in_=bias.rearrange("(i c) -> i c", i=BIAS_ROWS)
+        )
         a_raw = keep.tile([P, PACK * D_IN], BF16)
         nc.sync.dma_start(
             out=a_raw[:].rearrange("m (u r) -> m u r", u=HALVES),
@@ -118,11 +124,6 @@ def tile_replaced_compose_lora_pa_s_kernel(
         ident = keep.tile([P, P], F32)
         make_identity(nc, ident[:])
 
-        rows_bank = banks.tile([P, P], F32, tag="bank")
-        nc.tensor.transpose(rows_bank[:], rows[:].bitcast(F32), ident[:])
-        columns = keep.tile([P, WEIGHT_ROW + 1], F32)
-        nc.vector.tensor_copy(out=columns[:], in_=rows_bank[:, 0 : WEIGHT_ROW + 1])
-
         x_grouped = keep.tile([P, P * PACK], BF16, align_bytes=64)
         contraction_to_partitions(
             nc,
@@ -131,6 +132,11 @@ def tile_replaced_compose_lora_pa_s_kernel(
             row_blocks(x_raw),
             x_grouped[:].bitcast(F32).rearrange("w (b c u) -> w c b u", b=1, u=HALVES),
         )
+
+        rows_bank = banks.tile([P, P], F32, tag="bank")
+        nc.tensor.transpose(rows_bank[:], rows[:].bitcast(F32), ident[:])
+        columns = keep.tile([P, WEIGHT_ROW + 1], F32)
+        nc.vector.tensor_copy(out=columns[:], in_=rows_bank[:, 0 : WEIGHT_ROW + 1])
 
         weight_bank = banks.tile([P, P], F32, tag="bank")
         nc.tensor.transpose(
@@ -191,7 +197,7 @@ def tile_replaced_compose_lora_pa_s_kernel(
 
         scale_half(0)
         bc_banks = banks_for(banks, bc_blocks)
-        transpose_half(nc, bc_banks, ident, bc_blocks, 0)
+        transpose_half(nc, bc_banks, ident, bc_blocks, 0, 2)
 
         a_codes = keep.tile([P, PACK * P], U32, align_bytes=64)
         a_scales = keep.tile([P, PACK * P], U8, align_bytes=64)
@@ -213,23 +219,9 @@ def tile_replaced_compose_lora_pa_s_kernel(
             in_=h_bank[:].rearrange("p t s -> p s t"),
         )
 
-        scale_half(1)
-        transpose_half(nc, bc_banks, ident, bc_blocks, 1)
-
-        h_codes = keep.tile([P, P], U32, align_bytes=64)
-        h_scales = keep.tile([P, P], U8, align_bytes=64)
-        nc.vector.quantize_mx(out=h_codes[:].bitcast(FP8X4), scales=h_scales[:], in_=h_grouped[:])
-
-        b_grouped = keep.tile([P, D_OUT * PACK], BF16, align_bytes=64)
-        leave_banks(
-            bc_banks,
-            len(bc_blocks),
-            b_grouped[:].bitcast(F32).rearrange("w (c b u) -> w c b u", b=O_PER_PARTITION, u=HALVES),
-            [nc.scalar.copy, nc.vector.tensor_copy],
-        )
-
         w_grouped = keep.tile([P, D_OUT * PACK], BF16, align_bytes=64)
-        for g in range(OUT_CHUNKS):
+
+        def transpose_w_piece(g):
             contraction_to_partitions(
                 nc,
                 banks,
@@ -240,28 +232,50 @@ def tile_replaced_compose_lora_pa_s_kernel(
                 .rearrange("w (c b u) -> w c b u", b=ROWS_PER_PARTITION, u=HALVES),
             )
 
-        b_codes = keep.tile([P, D_OUT], U32, align_bytes=64)
-        b_scales = keep.tile([P, D_OUT], U8, align_bytes=64)
+        scale_half(1)
+        transpose_w_piece(0)
+        transpose_half(nc, bc_banks, ident, bc_blocks, 1, 2)
+
+        h_codes = keep.tile([P, P], U32, align_bytes=64)
+        h_scales = keep.tile([P, P], U8, align_bytes=64)
+        nc.vector.quantize_mx(out=h_codes[:].bitcast(FP8X4), scales=h_scales[:], in_=h_grouped[:])
+
         w_codes = keep.tile([P, D_OUT], U32, align_bytes=64)
         w_scales = keep.tile([P, D_OUT], U8, align_bytes=64)
-        out_sb = keep.tile([P, D_OUT], F32)
-        out_rows = out.flatten_outer_dims()
 
-        def quantise_piece(g):
+        def quantise_w_piece(g):
             cols = slice(g * N_TILE, (g + 1) * N_TILE)
-            values = slice(g * N_TILE * PACK, (g + 1) * N_TILE * PACK)
             nc.vector.quantize_mx(
-                out=b_codes[:, cols].bitcast(FP8X4), scales=b_scales[:, cols], in_=b_grouped[:, values]
-            )
-            nc.vector.quantize_mx(
-                out=w_codes[:, cols].bitcast(FP8X4), scales=w_scales[:, cols], in_=w_grouped[:, values]
+                out=w_codes[:, cols].bitcast(FP8X4),
+                scales=w_scales[:, cols],
+                in_=w_grouped[:, g * N_TILE * PACK : (g + 1) * N_TILE * PACK],
             )
 
-        def finish_piece(g):
+        quantise_w_piece(0)
+
+        b_grouped = keep.tile([P, D_OUT * PACK], BF16, align_bytes=64)
+        leave_banks(
+            bc_banks,
+            len(bc_blocks),
+            b_grouped[:].bitcast(F32).rearrange("w (c b u) -> w c b u", b=O_PER_PARTITION, u=HALVES),
+            [nc.scalar.copy, nc.vector.tensor_copy],
+        )
+        for g in range(1, OUT_CHUNKS):
+            transpose_w_piece(g)
+
+        b_codes = keep.tile([P, D_OUT], U32, align_bytes=64)
+        b_scales = keep.tile([P, D_OUT], U8, align_bytes=64)
+        acc = []
+        for g in range(OUT_CHUNKS):
             cols = slice(g * N_TILE, (g + 1) * N_TILE)
-            acc = banks.tile([P, N_TILE], F32, tag="bank")
+            nc.vector.quantize_mx(
+                out=b_codes[:, cols].bitcast(FP8X4),
+                scales=b_scales[:, cols],
+                in_=b_grouped[:, g * N_TILE * PACK : (g + 1) * N_TILE * PACK],
+            )
+            sums = banks.tile([P, N_TILE], F32, tag="bank", name="acc%d" % g)
             nc.tensor.matmul_mx(
-                out=acc[:],
+                out=sums[:],
                 lhsT=h_codes[:].bitcast(FP8X4),
                 lhsT_scale=h_scales[:],
                 rhs=b_codes[:, cols].bitcast(FP8X4),
@@ -269,8 +283,16 @@ def tile_replaced_compose_lora_pa_s_kernel(
                 start=True,
                 stop=False,
             )
+            acc.append(sums)
+        for g in range(1, OUT_CHUNKS):
+            quantise_w_piece(g)
+
+        out_sb = keep.tile([P, D_OUT], F32)
+        out_rows = out.flatten_outer_dims()
+        for g in range(OUT_CHUNKS):
+            cols = slice(g * N_TILE, (g + 1) * N_TILE)
             nc.tensor.matmul_mx(
-                out=acc[:],
+                out=acc[g][:],
                 lhsT=x_codes[:].bitcast(FP8X4),
                 lhsT_scale=x_scales[:],
                 rhs=w_codes[:, cols].bitcast(FP8X4),
@@ -279,12 +301,6 @@ def tile_replaced_compose_lora_pa_s_kernel(
                 stop=True,
             )
             nc.vector.tensor_tensor(
-                out=out_sb[:, cols], in0=acc[:], in1=bias_all[:, cols], op=mybir.AluOpType.add
+                out=out_sb[:, cols], in0=acc[g][:], in1=bias_all[:, cols], op=mybir.AluOpType.add
             )
             nc.sync.dma_start(out=out_rows[:, cols], in_=out_sb[:, cols])
-
-        quantise_piece(0)
-        for g in range(1, OUT_CHUNKS):
-            quantise_piece(g)
-            finish_piece(g - 1)
-        finish_piece(OUT_CHUNKS - 1)

@@ -10,25 +10,27 @@ U8 = mybir.dt.uint8
 FP8X4 = mybir.dt.float8_e4m3fn_x4
 
 P = 128
+TOKENS = 128
 D_IN = 512
 D_OUT = 1024
 ADAPTERS = 32
 RANK = 16
 LORA_SCALE = 2.0
 PACK = 4
+PAIR = 2
 HALVES = 2
 BLOCKS_PER_BANK = 2
 PSUM_BANKS = 8
 O_PER_PARTITION = D_OUT // P
 HALF_ADAPTERS = ADAPTERS // HALVES
 CHUNK_ADAPTERS = 8
-OUT_CHUNKS = 4
-N_TILE = D_OUT // OUT_CHUNKS
+PIECES = 4
+N_TILE = D_OUT // PIECES
 ROWS_PER_PARTITION = N_TILE // P
 BIAS_ROWS = 4
-WEIGHT_ROW = 4
+WEIGHT_ROW = BIAS_ROWS
 
-FLOPS = 2 * P * D_IN * (ADAPTERS * RANK + D_OUT) + 2 * P * ADAPTERS * RANK * D_OUT
+FLOPS = 2 * TOKENS * D_IN * (ADAPTERS * RANK + D_OUT) + 2 * TOKENS * ADAPTERS * RANK * D_OUT
 
 
 def banks_for(banks, blocks):
@@ -39,32 +41,26 @@ def banks_for(banks, blocks):
     return bank_tiles
 
 
-def dealt(n_banks, n_engines):
-    run = n_banks // n_engines
-    return [(e, e * run + i) for i in range(run) for e in range(n_engines)]
-
-
-def transpose_half(nc, bank_tiles, ident, blocks, u, n_engines):
-    for e, i in dealt(len(bank_tiles), n_engines):
-        first = i * BLOCKS_PER_BANK
-        for b in range(first, min(first + BLOCKS_PER_BANK, len(blocks))):
-            nc.tensor.transpose(bank_tiles[i][:, b - first, u, :], blocks[b][u], ident[:])
+def transpose_half(nc, bank_tiles, ident, blocks, u):
+    for b in range(len(blocks)):
+        bank = bank_tiles[b // BLOCKS_PER_BANK]
+        nc.tensor.transpose(bank[:, b % BLOCKS_PER_BANK, u, :], blocks[b][u], ident[:])
 
 
 def leave_banks(bank_tiles, n_blocks, places, copies):
-    for e, i in dealt(len(bank_tiles), len(copies)):
+    for i, bank in enumerate(bank_tiles):
         first = i * BLOCKS_PER_BANK
         count = min(BLOCKS_PER_BANK, n_blocks - first)
-        copies[e](
+        copies[i * len(copies) // len(bank_tiles)](
             out=places[:, :, first : first + count, :],
-            in_=bank_tiles[i][:, 0:count].rearrange("w b u c -> w c b u"),
+            in_=bank[:, 0:count].rearrange("w b u c -> w c b u"),
         )
 
 
 def contraction_to_partitions(nc, banks, ident, blocks, places):
     bank_tiles = banks_for(banks, blocks)
     for u in range(HALVES):
-        transpose_half(nc, bank_tiles, ident, blocks, u, 1)
+        transpose_half(nc, bank_tiles, ident, blocks, u)
     leave_banks(bank_tiles, len(blocks), places, [nc.scalar.copy])
 
 
@@ -82,21 +78,21 @@ def tile_replaced_compose_lora_pa_s_kernel(
         banks = stack.enter_context(tc.psum_pool(name="banks", bufs=PSUM_BANKS))
         stack.enter_context(tc.manual_schedule())
 
-        x_raw = keep.tile([P, D_IN], BF16)
+        x_raw = keep.tile([TOKENS, D_IN], BF16)
         nc.sync.dma_start(out=x_raw[:], in_=x.flatten_outer_dims())
-        rows = keep.tile([P, 2 * P], BF16)
-        nc.vector.memset(rows[:].bitcast(F32), 0.0)
+        small_rows = keep.tile([P, PAIR * P], BF16)
+        nc.vector.memset(small_rows[:].bitcast(F32), 0.0)
         nc.sync.dma_start(
-            out=rows[WEIGHT_ROW : WEIGHT_ROW + 1, 0:ADAPTERS],
+            out=small_rows[WEIGHT_ROW : WEIGHT_ROW + 1, 0:ADAPTERS],
             in_=lora_weights.rearrange("(o n) -> o n", o=1),
         )
         nc.sync.dma_start(
-            out=rows[0:BIAS_ROWS, :], in_=bias.rearrange("(i c) -> i c", i=BIAS_ROWS)
+            out=small_rows[0:BIAS_ROWS, :], in_=bias.rearrange("(i c) -> i c", i=BIAS_ROWS)
         )
         a_raw = keep.tile([P, PACK * D_IN], BF16)
         nc.sync.dma_start(
-            out=a_raw[:].rearrange("m (u r) -> m u r", u=HALVES),
-            in_=lora_A.flatten_outer_dims().rearrange("(u m e) d -> m u (e d)", u=HALVES, e=2),
+            out=a_raw[:].rearrange("w (u r) -> w u r", u=HALVES),
+            in_=lora_A.flatten_outer_dims().rearrange("(u w e) d -> w u (e d)", u=HALVES, e=PAIR),
         )
         b_raw = []
         for first in range(0, ADAPTERS, CHUNK_ADAPTERS):
@@ -111,7 +107,7 @@ def tile_replaced_compose_lora_pa_s_kernel(
             )
             b_raw.append(chunk)
         w_raw = []
-        for g in range(OUT_CHUNKS):
+        for g in range(PIECES):
             piece = keep.tile([P, ROWS_PER_PARTITION * D_IN], BF16, name="w_raw%d" % g)
             nc.sync.dma_start(
                 out=piece[:],
@@ -124,7 +120,7 @@ def tile_replaced_compose_lora_pa_s_kernel(
         ident = keep.tile([P, P], F32)
         make_identity(nc, ident[:])
 
-        x_grouped = keep.tile([P, P * PACK], BF16, align_bytes=64)
+        x_grouped = keep.tile([P, TOKENS * PACK], BF16, align_bytes=64)
         contraction_to_partitions(
             nc,
             banks,
@@ -133,26 +129,27 @@ def tile_replaced_compose_lora_pa_s_kernel(
             x_grouped[:].bitcast(F32).rearrange("w (b c u) -> w c b u", b=1, u=HALVES),
         )
 
-        rows_bank = banks.tile([P, P], F32, tag="bank")
-        nc.tensor.transpose(rows_bank[:], rows[:].bitcast(F32), ident[:])
-        columns = keep.tile([P, WEIGHT_ROW + 1], F32)
-        nc.vector.tensor_copy(out=columns[:], in_=rows_bank[:, 0 : WEIGHT_ROW + 1])
-
+        small_bank = banks.tile([P, P], F32, tag="bank")
+        nc.tensor.transpose(small_bank[:], small_rows[:].bitcast(F32), ident[:])
+        small_columns = keep.tile([P, WEIGHT_ROW + 1], F32)
+        nc.vector.tensor_copy(out=small_columns[:], in_=small_bank[:, 0 : WEIGHT_ROW + 1])
         weight_bank = banks.tile([P, P], F32, tag="bank")
         nc.tensor.transpose(
-            weight_bank[:], columns[:, WEIGHT_ROW : WEIGHT_ROW + 1].to_broadcast([P, P]), ident[:]
+            weight_bank[:],
+            small_columns[:, WEIGHT_ROW : WEIGHT_ROW + 1].to_broadcast([P, P]),
+            ident[:],
         )
         coef = keep.tile([P, ADAPTERS, RANK], BF16)
         nc.vector.tensor_scalar_mul(
             out=coef[:],
-            in0=weight_bank[:, 0 : ADAPTERS // 2]
+            in0=weight_bank[:, 0 : ADAPTERS // PAIR]
             .bitcast(BF16)
             .unsqueeze(2)
             .to_broadcast([P, ADAPTERS, RANK]),
             scalar1=LORA_SCALE,
         )
-        x_codes = keep.tile([P, P], U32, align_bytes=64)
-        x_scales = keep.tile([P, P], U8, align_bytes=64)
+        x_codes = keep.tile([P, TOKENS], U32, align_bytes=64)
+        x_scales = keep.tile([P, TOKENS], U8, align_bytes=64)
         nc.vector.quantize_mx(out=x_codes[:].bitcast(FP8X4), scales=x_scales[:], in_=x_grouped[:])
 
         a_grouped = keep.tile([P, PACK * P * PACK], BF16, align_bytes=64)
@@ -167,7 +164,7 @@ def tile_replaced_compose_lora_pa_s_kernel(
         bias_bank = banks.tile([P, BIAS_ROWS, P], F32, tag="bank")
         for i in range(BIAS_ROWS):
             nc.tensor.transpose(
-                bias_bank[:, i, :], columns[:, i : i + 1].to_broadcast([P, P]), ident[:]
+                bias_bank[:, i, :], small_columns[:, i : i + 1].to_broadcast([P, P]), ident[:]
             )
         bias_all = keep.tile([P, D_OUT], BF16)
         nc.scalar.copy(
@@ -180,8 +177,9 @@ def tile_replaced_compose_lora_pa_s_kernel(
             bc.append(half)
         bc_words = [half[:].bitcast(F32).rearrange("p (l w) -> p l w", w=P) for half in bc]
         bc_blocks = [[bc_words[u][:, l, :] for u in range(HALVES)] for l in range(O_PER_PARTITION)]
+        bc_banks = banks_for(banks, bc_blocks)
 
-        def scale_half(u):
+        def scale_and_transpose_half(u):
             for in_half in range(0, HALF_ADAPTERS, CHUNK_ADAPTERS):
                 first = u * HALF_ADAPTERS + in_half
                 nc.vector.tensor_tensor(
@@ -194,15 +192,14 @@ def tile_replaced_compose_lora_pa_s_kernel(
                     .to_broadcast([P, O_PER_PARTITION, CHUNK_ADAPTERS, RANK]),
                     op=mybir.AluOpType.mult,
                 )
+            transpose_half(nc, bc_banks, ident, bc_blocks, u)
 
-        scale_half(0)
-        bc_banks = banks_for(banks, bc_blocks)
-        transpose_half(nc, bc_banks, ident, bc_blocks, 0, 2)
+        scale_and_transpose_half(0)
 
         a_codes = keep.tile([P, PACK * P], U32, align_bytes=64)
         a_scales = keep.tile([P, PACK * P], U8, align_bytes=64)
         nc.vector.quantize_mx(out=a_codes[:].bitcast(FP8X4), scales=a_scales[:], in_=a_grouped[:])
-        h_bank = banks.tile([P, PACK, P], F32, tag="bank")
+        h_bank = banks.tile([P, PACK, TOKENS], F32, tag="bank")
         for t in range(PACK):
             nc.tensor.matmul_mx(
                 out=h_bank[:, t, :],
@@ -213,15 +210,28 @@ def tile_replaced_compose_lora_pa_s_kernel(
                 start=True,
                 stop=True,
             )
-        h_grouped = keep.tile([P, P * PACK], BF16, align_bytes=64)
+        h_grouped = keep.tile([P, TOKENS * PACK], BF16, align_bytes=64)
         nc.scalar.copy(
-            out=h_grouped[:].rearrange("p (s t) -> p s t", t=PACK),
-            in_=h_bank[:].rearrange("p t s -> p s t"),
+            out=h_grouped[:].rearrange("w (s t) -> w s t", t=PACK),
+            in_=h_bank[:].rearrange("w t s -> w s t"),
+        )
+
+        scale_and_transpose_half(1)
+
+        h_codes = keep.tile([P, TOKENS], U32, align_bytes=64)
+        h_scales = keep.tile([P, TOKENS], U8, align_bytes=64)
+        nc.vector.quantize_mx(out=h_codes[:].bitcast(FP8X4), scales=h_scales[:], in_=h_grouped[:])
+
+        b_grouped = keep.tile([P, D_OUT * PACK], BF16, align_bytes=64)
+        leave_banks(
+            bc_banks,
+            len(bc_blocks),
+            b_grouped[:].bitcast(F32).rearrange("w (c b u) -> w c b u", b=O_PER_PARTITION, u=HALVES),
+            [nc.scalar.copy, nc.vector.tensor_copy],
         )
 
         w_grouped = keep.tile([P, D_OUT * PACK], BF16, align_bytes=64)
-
-        def transpose_w_piece(g):
+        for g in range(PIECES):
             contraction_to_partitions(
                 nc,
                 banks,
@@ -232,48 +242,17 @@ def tile_replaced_compose_lora_pa_s_kernel(
                 .rearrange("w (c b u) -> w c b u", b=ROWS_PER_PARTITION, u=HALVES),
             )
 
-        scale_half(1)
-        transpose_w_piece(0)
-        transpose_half(nc, bc_banks, ident, bc_blocks, 1, 2)
-
-        h_codes = keep.tile([P, P], U32, align_bytes=64)
-        h_scales = keep.tile([P, P], U8, align_bytes=64)
-        nc.vector.quantize_mx(out=h_codes[:].bitcast(FP8X4), scales=h_scales[:], in_=h_grouped[:])
-
-        w_codes = keep.tile([P, D_OUT], U32, align_bytes=64)
-        w_scales = keep.tile([P, D_OUT], U8, align_bytes=64)
-
-        def quantise_w_piece(g):
-            cols = slice(g * N_TILE, (g + 1) * N_TILE)
-            nc.vector.quantize_mx(
-                out=w_codes[:, cols].bitcast(FP8X4),
-                scales=w_scales[:, cols],
-                in_=w_grouped[:, g * N_TILE * PACK : (g + 1) * N_TILE * PACK],
-            )
-
-        quantise_w_piece(0)
-
-        b_grouped = keep.tile([P, D_OUT * PACK], BF16, align_bytes=64)
-        leave_banks(
-            bc_banks,
-            len(bc_blocks),
-            b_grouped[:].bitcast(F32).rearrange("w (c b u) -> w c b u", b=O_PER_PARTITION, u=HALVES),
-            [nc.scalar.copy, nc.vector.tensor_copy],
-        )
-        for g in range(1, OUT_CHUNKS):
-            transpose_w_piece(g)
-
         b_codes = keep.tile([P, D_OUT], U32, align_bytes=64)
         b_scales = keep.tile([P, D_OUT], U8, align_bytes=64)
         acc = []
-        for g in range(OUT_CHUNKS):
+        for g in range(PIECES):
             cols = slice(g * N_TILE, (g + 1) * N_TILE)
             nc.vector.quantize_mx(
                 out=b_codes[:, cols].bitcast(FP8X4),
                 scales=b_scales[:, cols],
                 in_=b_grouped[:, g * N_TILE * PACK : (g + 1) * N_TILE * PACK],
             )
-            sums = banks.tile([P, N_TILE], F32, tag="bank", name="acc%d" % g)
+            sums = banks.tile([TOKENS, N_TILE], F32, tag="bank", name="acc%d" % g)
             nc.tensor.matmul_mx(
                 out=sums[:],
                 lhsT=h_codes[:].bitcast(FP8X4),
@@ -284,12 +263,20 @@ def tile_replaced_compose_lora_pa_s_kernel(
                 stop=False,
             )
             acc.append(sums)
-        for g in range(1, OUT_CHUNKS):
-            quantise_w_piece(g)
 
-        out_sb = keep.tile([P, D_OUT], F32)
+        w_codes = keep.tile([P, D_OUT], U32, align_bytes=64)
+        w_scales = keep.tile([P, D_OUT], U8, align_bytes=64)
+        for g in range(PIECES):
+            cols = slice(g * N_TILE, (g + 1) * N_TILE)
+            nc.vector.quantize_mx(
+                out=w_codes[:, cols].bitcast(FP8X4),
+                scales=w_scales[:, cols],
+                in_=w_grouped[:, g * N_TILE * PACK : (g + 1) * N_TILE * PACK],
+            )
+
+        out_sb = keep.tile([TOKENS, D_OUT], F32)
         out_rows = out.flatten_outer_dims()
-        for g in range(OUT_CHUNKS):
+        for g in range(PIECES):
             cols = slice(g * N_TILE, (g + 1) * N_TILE)
             nc.tensor.matmul_mx(
                 out=acc[g][:],

@@ -23,7 +23,7 @@ BLOCKS_PER_BANK = 2
 PSUM_BANKS = 8
 O_PER_PARTITION = D_OUT // P
 HALF_ADAPTERS = ADAPTERS // HALVES
-CHUNK_ADAPTERS = 8
+CHUNK_ADAPTERS = 4
 PIECES = 4
 N_TILE = D_OUT // PIECES
 ROWS_PER_PARTITION = N_TILE // P

from contextlib import ExitStack

import concourse.mybir as mybir
from concourse.masks import make_identity

F32 = mybir.dt.float32
BF16 = mybir.dt.bfloat16
U32 = mybir.dt.uint32
U8 = mybir.dt.uint8
FP8X4 = mybir.dt.float8_e4m3fn_x4

P = 128
TOKENS = 128
D_IN = 512
D_OUT = 1024
ADAPTERS = 32
RANK = 16
LORA_SCALE = 2.0
PACK = 4
PAIR = 2
HALVES = 2
BLOCKS_PER_BANK = 2
PSUM_BANKS = 8
O_PER_PARTITION = D_OUT // P
HALF_ADAPTERS = ADAPTERS // HALVES
CHUNK_ADAPTERS = 4
PIECES = 4
N_TILE = D_OUT // PIECES
ROWS_PER_PARTITION = N_TILE // P
BIAS_ROWS = 4
WEIGHT_ROW = BIAS_ROWS

FLOPS = 2 * TOKENS * D_IN * (ADAPTERS * RANK + D_OUT) + 2 * TOKENS * ADAPTERS * RANK * D_OUT


def banks_for(banks, blocks):
    bank_tiles = []
    for first in range(0, len(blocks), BLOCKS_PER_BANK):
        bank = banks.tile([P, BLOCKS_PER_BANK, HALVES, P], F32, tag="bank")
        bank_tiles.append(bank)
    return bank_tiles


def transpose_half(nc, bank_tiles, ident, blocks, u):
    for b in range(len(blocks)):
        bank = bank_tiles[b // BLOCKS_PER_BANK]
        nc.tensor.transpose(bank[:, b % BLOCKS_PER_BANK, u, :], blocks[b][u], ident[:])


def leave_banks(bank_tiles, n_blocks, places, copies):
    for i, bank in enumerate(bank_tiles):
        first = i * BLOCKS_PER_BANK
        count = min(BLOCKS_PER_BANK, n_blocks - first)
        copies[i * len(copies) // len(bank_tiles)](
            out=places[:, :, first : first + count, :],
            in_=bank[:, 0:count].rearrange("w b u c -> w c b u"),
        )


def contraction_to_partitions(nc, banks, ident, blocks, places):
    bank_tiles = banks_for(banks, blocks)
    for u in range(HALVES):
        transpose_half(nc, bank_tiles, ident, blocks, u)
    leave_banks(bank_tiles, len(blocks), places, [nc.scalar.copy])


def row_blocks(raw):
    words = raw[:].bitcast(F32).rearrange("p (b u w) -> p b u w", u=HALVES, w=P)
    return [[words[:, b, u, :] for u in range(HALVES)] for b in range(words.shape[1])]


def tile_replaced_compose_lora_pa_s_kernel(
    tc, x, lora_A, lora_B, W, bias, lora_weights, out
):
    nc = tc.nc
    with ExitStack() as stack:
        keep = stack.enter_context(tc.tile_pool(name="keep", bufs=1))
        banks = stack.enter_context(tc.psum_pool(name="banks", bufs=PSUM_BANKS))
        stack.enter_context(tc.manual_schedule())

        x_raw = keep.tile([TOKENS, D_IN], BF16)
        nc.sync.dma_start(out=x_raw[:], in_=x.flatten_outer_dims())
        small_rows = keep.tile([P, PAIR * P], BF16)
        nc.vector.memset(small_rows[:].bitcast(F32), 0.0)
        nc.sync.dma_start(
            out=small_rows[WEIGHT_ROW : WEIGHT_ROW + 1, 0:ADAPTERS],
            in_=lora_weights.rearrange("(o n) -> o n", o=1),
        )
        nc.sync.dma_start(
            out=small_rows[0:BIAS_ROWS, :], in_=bias.rearrange("(i c) -> i c", i=BIAS_ROWS)
        )
        a_raw = keep.tile([P, PACK * D_IN], BF16)
        nc.sync.dma_start(
            out=a_raw[:].rearrange("w (u r) -> w u r", u=HALVES),
            in_=lora_A.flatten_outer_dims().rearrange("(u w e) d -> w u (e d)", u=HALVES, e=PAIR),
        )
        b_raw = []
        for first in range(0, ADAPTERS, CHUNK_ADAPTERS):
            chunk = keep.tile(
                [P, CHUNK_ADAPTERS, O_PER_PARTITION * RANK], BF16, name="b_raw%d" % first
            )
            nc.sync.dma_start(
                out=chunk[:],
                in_=lora_B[first : first + CHUNK_ADAPTERS].rearrange(
                    "n (p l) r -> p n (l r)", l=O_PER_PARTITION
                ),
            )
            b_raw.append(chunk)
        w_raw = []
        for g in range(PIECES):
            piece = keep.tile([P, ROWS_PER_PARTITION * D_IN], BF16, name="w_raw%d" % g)
            nc.sync.dma_start(
                out=piece[:],
                in_=W[g * N_TILE : (g + 1) * N_TILE, :].rearrange(
                    "(q j) d -> q (j d)", j=ROWS_PER_PARTITION
                ),
            )
            w_raw.append(piece)

        ident = keep.tile([P, P], F32)
        make_identity(nc, ident[:])

        x_grouped = keep.tile([P, TOKENS * PACK], BF16, align_bytes=64)
        contraction_to_partitions(
            nc,
            banks,
            ident,
            row_blocks(x_raw),
            x_grouped[:].bitcast(F32).rearrange("w (b c u) -> w c b u", b=1, u=HALVES),
        )

        small_bank = banks.tile([P, P], F32, tag="bank")
        nc.tensor.transpose(small_bank[:], small_rows[:].bitcast(F32), ident[:])
        small_columns = keep.tile([P, WEIGHT_ROW + 1], F32)
        nc.vector.tensor_copy(out=small_columns[:], in_=small_bank[:, 0 : WEIGHT_ROW + 1])
        weight_bank = banks.tile([P, P], F32, tag="bank")
        nc.tensor.transpose(
            weight_bank[:],
            small_columns[:, WEIGHT_ROW : WEIGHT_ROW + 1].to_broadcast([P, P]),
            ident[:],
        )
        coef = keep.tile([P, ADAPTERS, RANK], BF16)
        nc.vector.tensor_scalar_mul(
            out=coef[:],
            in0=weight_bank[:, 0 : ADAPTERS // PAIR]
            .bitcast(BF16)
            .unsqueeze(2)
            .to_broadcast([P, ADAPTERS, RANK]),
            scalar1=LORA_SCALE,
        )
        x_codes = keep.tile([P, TOKENS], U32, align_bytes=64)
        x_scales = keep.tile([P, TOKENS], U8, align_bytes=64)
        nc.vector.quantize_mx(out=x_codes[:].bitcast(FP8X4), scales=x_scales[:], in_=x_grouped[:])

        a_grouped = keep.tile([P, PACK * P * PACK], BF16, align_bytes=64)
        contraction_to_partitions(
            nc,
            banks,
            ident,
            row_blocks(a_raw),
            a_grouped[:].bitcast(F32).rearrange("w (b c u) -> w c b u", b=PACK, u=HALVES),
        )

        bias_bank = banks.tile([P, BIAS_ROWS, P], F32, tag="bank")
        for i in range(BIAS_ROWS):
            nc.tensor.transpose(
                bias_bank[:, i, :], small_columns[:, i : i + 1].to_broadcast([P, P]), ident[:]
            )
        bias_all = keep.tile([P, D_OUT], BF16)
        nc.scalar.copy(
            out=bias_all[:].bitcast(F32), in_=bias_bank[:].rearrange("p i w -> p (i w)")
        )

        bc = []
        for u in range(HALVES):
            half = keep.tile([P, O_PER_PARTITION * HALF_ADAPTERS * RANK], BF16, name="bc%d" % u)
            bc.append(half)
        bc_words = [half[:].bitcast(F32).rearrange("p (l w) -> p l w", w=P) for half in bc]
        bc_blocks = [[bc_words[u][:, l, :] for u in range(HALVES)] for l in range(O_PER_PARTITION)]
        bc_banks = banks_for(banks, bc_blocks)

        def scale_and_transpose_half(u):
            for in_half in range(0, HALF_ADAPTERS, CHUNK_ADAPTERS):
                first = u * HALF_ADAPTERS + in_half
                nc.vector.tensor_tensor(
                    out=bc[u][:].rearrange("p (l n r) -> p l n r", l=O_PER_PARTITION, r=RANK)[
                        :, :, in_half : in_half + CHUNK_ADAPTERS, :
                    ],
                    in0=b_raw[first // CHUNK_ADAPTERS][:].rearrange("p n (l r) -> p l n r", r=RANK),
                    in1=coef[:, first : first + CHUNK_ADAPTERS, :]
                    .unsqueeze(1)
                    .to_broadcast([P, O_PER_PARTITION, CHUNK_ADAPTERS, RANK]),
                    op=mybir.AluOpType.mult,
                )
            transpose_half(nc, bc_banks, ident, bc_blocks, u)

        scale_and_transpose_half(0)

        a_codes = keep.tile([P, PACK * P], U32, align_bytes=64)
        a_scales = keep.tile([P, PACK * P], U8, align_bytes=64)
        nc.vector.quantize_mx(out=a_codes[:].bitcast(FP8X4), scales=a_scales[:], in_=a_grouped[:])
        h_bank = banks.tile([P, PACK, TOKENS], F32, tag="bank")
        for t in range(PACK):
            nc.tensor.matmul_mx(
                out=h_bank[:, t, :],
                lhsT=a_codes[:, t * P : (t + 1) * P].bitcast(FP8X4),
                lhsT_scale=a_scales[:, t * P : (t + 1) * P],
                rhs=x_codes[:].bitcast(FP8X4),
                rhs_scale=x_scales[:],
                start=True,
                stop=True,
            )
        h_grouped = keep.tile([P, TOKENS * PACK], BF16, align_bytes=64)
        nc.scalar.copy(
            out=h_grouped[:].rearrange("w (s t) -> w s t", t=PACK),
            in_=h_bank[:].rearrange("w t s -> w s t"),
        )

        scale_and_transpose_half(1)

        h_codes = keep.tile([P, TOKENS], U32, align_bytes=64)
        h_scales = keep.tile([P, TOKENS], U8, align_bytes=64)
        nc.vector.quantize_mx(out=h_codes[:].bitcast(FP8X4), scales=h_scales[:], in_=h_grouped[:])

        b_grouped = keep.tile([P, D_OUT * PACK], BF16, align_bytes=64)
        leave_banks(
            bc_banks,
            len(bc_blocks),
            b_grouped[:].bitcast(F32).rearrange("w (c b u) -> w c b u", b=O_PER_PARTITION, u=HALVES),
            [nc.scalar.copy, nc.vector.tensor_copy],
        )

        w_grouped = keep.tile([P, D_OUT * PACK], BF16, align_bytes=64)
        for g in range(PIECES):
            contraction_to_partitions(
                nc,
                banks,
                ident,
                row_blocks(w_raw[g]),
                w_grouped[:, g * N_TILE * PACK : (g + 1) * N_TILE * PACK]
                .bitcast(F32)
                .rearrange("w (c b u) -> w c b u", b=ROWS_PER_PARTITION, u=HALVES),
            )

        b_codes = keep.tile([P, D_OUT], U32, align_bytes=64)
        b_scales = keep.tile([P, D_OUT], U8, align_bytes=64)
        acc = []
        for g in range(PIECES):
            cols = slice(g * N_TILE, (g + 1) * N_TILE)
            nc.vector.quantize_mx(
                out=b_codes[:, cols].bitcast(FP8X4),
                scales=b_scales[:, cols],
                in_=b_grouped[:, g * N_TILE * PACK : (g + 1) * N_TILE * PACK],
            )
            sums = banks.tile([TOKENS, N_TILE], F32, tag="bank", name="acc%d" % g)
            nc.tensor.matmul_mx(
                out=sums[:],
                lhsT=h_codes[:].bitcast(FP8X4),
                lhsT_scale=h_scales[:],
                rhs=b_codes[:, cols].bitcast(FP8X4),
                rhs_scale=b_scales[:, cols],
                start=True,
                stop=False,
            )
            acc.append(sums)

        w_codes = keep.tile([P, D_OUT], U32, align_bytes=64)
        w_scales = keep.tile([P, D_OUT], U8, align_bytes=64)
        for g in range(PIECES):
            cols = slice(g * N_TILE, (g + 1) * N_TILE)
            nc.vector.quantize_mx(
                out=w_codes[:, cols].bitcast(FP8X4),
                scales=w_scales[:, cols],
                in_=w_grouped[:, g * N_TILE * PACK : (g + 1) * N_TILE * PACK],
            )

        out_sb = keep.tile([TOKENS, D_OUT], F32)
        out_rows = out.flatten_outer_dims()
        for g in range(PIECES):
            cols = slice(g * N_TILE, (g + 1) * N_TILE)
            nc.tensor.matmul_mx(
                out=acc[g][:],
                lhsT=x_codes[:].bitcast(FP8X4),
                lhsT_scale=x_scales[:],
                rhs=w_codes[:, cols].bitcast(FP8X4),
                rhs_scale=w_scales[:, cols],
                start=False,
                stop=True,
            )
            nc.vector.tensor_tensor(
                out=out_sb[:, cols], in0=acc[g][:], in1=bias_all[:, cols], op=mybir.AluOpType.add
            )
            nc.sync.dma_start(out=out_rows[:, cols], in_=out_sb[:, cols])
